import numpy as np
import ml_dtypes


def mxq(x, axis, fmt="e4m3"):
    dtype, down = {"e4m3": (ml_dtypes.float8_e4m3fn, 7), "e5m2": (ml_dtypes.float8_e5m2, 14)}[fmt]
    v = np.moveaxis(np.asarray(x, np.float32).astype(ml_dtypes.bfloat16).astype(np.float64), axis, -1)
    blocks = v.reshape(v.shape[:-1] + (-1, 32))
    amax = np.abs(blocks).max(-1, keepdims=True)
    byte = np.maximum(np.where(amax > 0, np.frexp(amax)[1] - 1 + 127, 0) - down, 1)
    scale = np.exp2(byte - 127.0)
    codes = (blocks / scale).astype(np.float32).astype(dtype).astype(np.float64)
    return np.moveaxis((codes * scale).reshape(v.shape), -1, axis)


WIDE = False


def mx_kscale(k):
    if not WIDE:
        return np.ones(k)
    levels = np.array([10, -10, 5, -5, 0])
    a = np.random.permutation(np.resize(levels, k // 512 * 4)).reshape(k // 512, 4)
    idx = np.arange(k)
    return np.exp2(a[idx // 512, idx % 128 // 32])


BF16 = ml_dtypes.bfloat16


def bf(x):
    return np.asarray(x, np.float32).astype(BF16)


def f64(x):
    return np.asarray(x).astype(np.float64)


N, I, O = 512, 2048, 2048


def setup_inputs():
    s = mx_kscale(I)
    mask = np.tile(np.array([0.0, 0.0, 1.0, 1.0]), I // 4)
    gd = mask + 0.1 * (1.0 - mask)
    gs = (1.0 - mask) + 0.1 * mask
    x = np.random.standard_normal((N, I)) * s
    wd = np.random.standard_normal((O, I)) * gd / np.sqrt(I) / s
    ws = np.random.standard_normal((O, I)) * gs / np.sqrt(I) / s
    return {"x": bf(x), "W_dense": bf(wd), "W_sparse": bf(ws)}


def reference(x, W_dense, W_sparse):
    xq = mxq(f64(x), 1, "e4m3")
    out_dense = xq @ mxq(f64(W_dense), 1, "e4m3").T
    out_sparse = xq @ mxq(f64(W_sparse), 1, "e4m3").T
    return out_dense + out_sparse

@@ -1,0 +1,181 @@
+from contextlib import ExitStack
+
+import concourse.mybir as mybir
+from concourse.masks import make_identity
+
+FP8X4 = mybir.dt.float8_e4m3fn_x4
+BF16 = mybir.dt.bfloat16
+F32 = mybir.dt.float32
+U32 = mybir.dt.uint32
+U8 = mybir.dt.uint8
+
+P = 128
+TOKENS = 512
+K = 2048
+OUTS = 2048
+FLOPS = 2 * 2 * TOKENS * K * OUTS
+
+CHUNKS = (128, 128, 256, 512, 512, 512)
+RAW_BUFS = 28
+GRP_BUFS = 4
+COD_BUFS = 8
+OT_BUFS = 8
+T_BANKS = 6
+ACC_BANKS = 2
+V_EVERY = 2
+
+
+def tile_myinterleavedmodule_kernel(tc, x, W_dense, W_sparse, out):
+    nc = tc.nc
+    weights = (W_dense, W_sparse)
+    with ExitStack() as ctx:
+        const = ctx.enter_context(tc.tile_pool(name="const", bufs=1))
+        rawp = ctx.enter_context(tc.tile_pool(name="rawp", bufs=RAW_BUFS))
+        grpp = ctx.enter_context(tc.tile_pool(name="grpp", bufs=GRP_BUFS))
+        codp = ctx.enter_context(tc.tile_pool(name="codp", bufs=COD_BUFS))
+        otp = ctx.enter_context(tc.tile_pool(name="otp", bufs=OT_BUFS))
+        tpool = ctx.enter_context(tc.psum_pool(name="tpool", bufs=T_BANKS))
+        apool = ctx.enter_context(tc.psum_pool(name="apool", bufs=ACC_BANKS))
+        ctx.enter_context(tc.manual_schedule())
+
+        ident = const.tile([P, P], F32, name="ident")
+        make_identity(nc, ident[:])
+        xcod = const.tile([P, 2048], U32, name="xcod", align_bytes=64)
+        xscl = const.tile([P, 2048], U8, name="xscl", align_bytes=64)
+
+        sources = [x[P * m : P * (m + 1), :] for m in range(4)]
+        first_tile = []
+        col0 = 0
+        for n in CHUNKS:
+            first_tile.append(len(sources))
+            for w in range(2):
+                for s in range(n // P):
+                    sources.append(weights[w][col0 + P * s : col0 + P * (s + 1), :])
+            col0 += n
+        raw_tiles = []
+        counts = {"transposed": 0, "banks": 0}
+
+        def load_more():
+            while len(raw_tiles) < min(len(sources), counts["transposed"] + RAW_BUFS):
+                t = rawp.tile([P, K], BF16, name="raw", tag="raw")
+                nc.sync.dma_start(out=t[:], in_=sources[len(raw_tiles)])
+                raw_tiles.append(t)
+
+        def transpose_tile(idx, n, w, s, grps):
+            per_unit = 1024 // n
+            rawf = raw_tiles[idx][:].bitcast(F32)
+            for gp in range(2):
+                ag = 4 * w + 2 * gp
+                unit = ag // per_unit
+                a0 = ag % per_unit
+                if unit not in grps:
+                    grps[unit] = grpp.tile([P, 4096], BF16, name="grp", tag="grp", align_bytes=64)
+                tp = tpool.tile([P, 512], F32, name="tp", tag="tp")
+                for q in range(4):
+                    j = 4 * gp + q
+                    nc.tensor.transpose(
+                        out=tp[:, P * q : P * (q + 1)],
+                        in_=rawf[:, P * j : P * (j + 1)],
+                        identity=ident[:],
+                    )
+                src = tp[:].rearrange("p (g u o) -> p g o u", g=2, u=2)
+                grpf = grps[unit][:].bitcast(F32).rearrange("p (a o u) -> p a o u", a=per_unit, o=n, u=2)
+                dst = grpf[:, a0 : a0 + 2, P * s : P * (s + 1), :]
+                if counts["banks"] % V_EVERY == V_EVERY - 1:
+                    nc.vector.tensor_copy(out=dst, in_=src)
+                else:
+                    nc.scalar.copy(out=dst, in_=src)
+                counts["banks"] += 1
+            counts["transposed"] += 1
+
+        load_more()
+        for pair in range(2):
+            grps = {}
+            for mh in range(2):
+                m = 2 * pair + mh
+                transpose_tile(m, P, mh, 0, grps)
+                nc.vector.quantize_mx(
+                    out=xcod[:, 512 * m : 512 * (m + 1)].bitcast(FP8X4),
+                    scales=xscl[:, 512 * m : 512 * (m + 1)],
+                    in_=grps[0][:, 2048 * mh : 2048 * (mh + 1)],
+                )
+        load_more()
+
+        units = {}
+
+        def transpose_run(c):
+            n = CHUNKS[c]
+            grps = {}
+            idx = first_tile[c]
+            cods = {}
+            for w in range(2):
+                for s in range(n // P):
+                    transpose_tile(idx, n, w, s, grps)
+                    idx += 1
+                if n == P:
+                    if w == 0:
+                        cods[0] = (
+                            codp.tile([P, 1024], U32, name="cod", tag="cod", align_bytes=64),
+                            codp.tile([P, 1024], U8, name="scl", tag="scl", align_bytes=64),
+                        )
+                    nc.vector.quantize_mx(
+                        out=cods[0][0][:, 512 * w : 512 * (w + 1)].bitcast(FP8X4),
+                        scales=cods[0][1][:, 512 * w : 512 * (w + 1)],
+                        in_=grps[0][:, 2048 * w : 2048 * (w + 1)],
+                    )
+            if n != P:
+                for unit in range(8 * n // 1024):
+                    cods[unit] = (
+                        codp.tile([P, 1024], U32, name="cod", tag="cod", align_bytes=64),
+                        codp.tile([P, 1024], U8, name="scl", tag="scl", align_bytes=64),
+                    )
+                    nc.vector.quantize_mx(
+                        out=cods[unit][0][:].bitcast(FP8X4),
+                        scales=cods[unit][1][:],
+                        in_=grps[unit][:],
+                    )
+            units[c] = cods
+            load_more()
+
+        starts = []
+        col0 = 0
+        for n in CHUNKS:
+            starts.append(col0)
+            col0 += n
+        ots = {}
+
+        def mx_run(c):
+            n = CHUNKS[c]
+            per_unit = 1024 // n
+            grp512 = starts[c] // 512
+            off = starts[c] % 512
+            for m in range(4):
+                acc = apool.tile([P, 512], F32, name="acc", tag="acc")
+                for ag in range(8):
+                    g = ag % 4
+                    cod, scl = units[c][ag // per_unit]
+                    a = ag % per_unit
+                    xs = slice(512 * m + P * g, 512 * m + P * (g + 1))
+                    nc.tensor.matmul_mx(
+                        out=acc[:, 0:n],
+                        lhsT=xcod[:, xs].bitcast(FP8X4),
+                        lhsT_scale=xscl[:, xs],
+                        rhs=cod[:, a * n : (a + 1) * n].bitcast(FP8X4),
+                        rhs_scale=scl[:, a * n : (a + 1) * n],
+                        start=(ag == 0),
+                        stop=(ag == 7),
+                    )
+                if off == 0:
+                    ots[(grp512, m)] = otp.tile([P, 512], F32, name="ot", tag="ot")
+                ot = ots[(grp512, m)]
+                nc.scalar.copy(out=ot[:, off : off + n], in_=acc[:, 0:n])
+                if off + n == 512:
+                    nc.sync.dma_start(
+                        out=out[P * m : P * (m + 1), 512 * grp512 : 512 * (grp512 + 1)], in_=ot[:]
+                    )
+
+        transpose_run(0)
+        for c in range(len(CHUNKS)):
+            if c + 1 < len(CHUNKS):
+                transpose_run(c + 1)
+            mx_run(c)

@@ -15,7 +15,7 @@ K = 2048
 OUTS = 2048
 FLOPS = 2 * 2 * TOKENS * K * OUTS
 
-CHUNKS = (128, 128, 256, 512, 512, 512)
+CHUNKS = (128, 128, 256, 256, 256, 512, 512)
 RAW_BUFS = 28
 GRP_BUFS = 4
 COD_BUFS = 8

@@ -28,6 +28,15 @@ V_EVERY = 2
 def tile_myinterleavedmodule_kernel(tc, x, W_dense, W_sparse, out):
     nc = tc.nc
     weights = (W_dense, W_sparse)
+    starts = [sum(CHUNKS[:c]) for c in range(len(CHUNKS))]
+
+    def chunk_tiles(c):
+        return [(c, w, s) for w in range(2) for s in range(CHUNKS[c] // P)]
+
+    load_order = [("x", 0, 0)] + chunk_tiles(0) + [("x", m, 0) for m in range(1, 4)]
+    for c in range(1, len(CHUNKS)):
+        load_order.extend(chunk_tiles(c))
+
     with ExitStack() as ctx:
         const = ctx.enter_context(tc.tile_pool(name="const", bufs=1))
         rawp = ctx.enter_context(tc.tile_pool(name="rawp", bufs=RAW_BUFS))
@@ -40,36 +49,57 @@ def tile_myinterleavedmodule_kernel(tc, x, W_dense, W_sparse, out):
 
         ident = const.tile([P, P], F32, name="ident")
         make_identity(nc, ident[:])
-        xcod = const.tile([P, 2048], U32, name="xcod", align_bytes=64)
-        xscl = const.tile([P, 2048], U8, name="xscl", align_bytes=64)
+        xcod = [const.tile([P, 512], U32, name="xcod%d" % m, align_bytes=64) for m in range(4)]
+        xscl = [const.tile([P, 512], U8, name="xscl%d" % m, align_bytes=64) for m in range(4)]
 
-        sources = [x[P * m : P * (m + 1), :] for m in range(4)]
-        first_tile = []
-        col0 = 0
-        for n in CHUNKS:
-            first_tile.append(len(sources))
-            for w in range(2):
-                for s in range(n // P):
-                    sources.append(weights[w][col0 + P * s : col0 + P * (s + 1), :])
-            col0 += n
-        raw_tiles = []
-        counts = {"transposed": 0, "banks": 0}
+        raw_tiles = {}
+        counts = {"transposed": 0, "banks": 0, "flushed": 0}
+        grps = {}
+        cods = {}
+        pending = []
+        ots = {}
 
         def load_more():
-            while len(raw_tiles) < min(len(sources), counts["transposed"] + RAW_BUFS):
+            while len(raw_tiles) < min(len(load_order), counts["transposed"] + RAW_BUFS):
+                key = load_order[len(raw_tiles)]
                 t = rawp.tile([P, K], BF16, name="raw", tag="raw")
-                nc.sync.dma_start(out=t[:], in_=sources[len(raw_tiles)])
-                raw_tiles.append(t)
+                if key[0] == "x":
+                    src = x[P * key[1] : P * (key[1] + 1), :]
+                else:
+                    row0 = starts[key[0]] + P * key[2]
+                    src = weights[key[1]][row0 : row0 + P, :]
+                nc.sync.dma_start(out=t[:], in_=src)
+                raw_tiles[key] = t
 
-        def transpose_tile(idx, n, w, s, grps):
+        def new_codes(c, unit):
+            cods[(c, unit)] = (
+                codp.tile([P, 1024], U32, name="cod", tag="cod", align_bytes=64),
+                codp.tile([P, 1024], U8, name="scl", tag="scl", align_bytes=64),
+            )
+
+        def flush_quantises():
+            for c, unit in pending[counts["flushed"] :]:
+                new_codes(c, unit)
+                nc.vector.quantize_mx(
+                    out=cods[(c, unit)][0][:].bitcast(FP8X4),
+                    scales=cods[(c, unit)][1][:],
+                    in_=grps[(c, unit)][:],
+                )
+            counts["flushed"] = len(pending)
+
+        def transpose_tile(key):
+            if key[0] == "x":
+                owner, n, w, s = ("x", key[1] // 2), P, key[1] % 2, 0
+            else:
+                owner, n, w, s = key[0], CHUNKS[key[0]], key[1], key[2]
             per_unit = 1024 // n
-            rawf = raw_tiles[idx][:].bitcast(F32)
+            rawf = raw_tiles[key][:].bitcast(F32)
             for gp in range(2):
                 ag = 4 * w + 2 * gp
                 unit = ag // per_unit
                 a0 = ag % per_unit
-                if unit not in grps:
-                    grps[unit] = grpp.tile([P, 4096], BF16, name="grp", tag="grp", align_bytes=64)
+                if (owner, unit) not in grps:
+                    grps[(owner, unit)] = grpp.tile([P, 4096], BF16, name="grp", tag="grp", align_bytes=64)
                 tp = tpool.tile([P, 512], F32, name="tp", tag="tp")
                 for q in range(4):
                     j = 4 * gp + q
@@ -79,7 +109,9 @@ def tile_myinterleavedmodule_kernel(tc, x, W_dense, W_sparse, out):
                         identity=ident[:],
                     )
                 src = tp[:].rearrange("p (g u o) -> p g o u", g=2, u=2)
-                grpf = grps[unit][:].bitcast(F32).rearrange("p (a o u) -> p a o u", a=per_unit, o=n, u=2)
+                grpf = grps[(owner, unit)][:].bitcast(F32).rearrange(
+                    "p (a o u) -> p a o u", a=per_unit, o=n, u=2
+                )
                 dst = grpf[:, a0 : a0 + 2, P * s : P * (s + 1), :]
                 if counts["banks"] % V_EVERY == V_EVERY - 1:
                     nc.vector.tensor_copy(out=dst, in_=src)
@@ -87,95 +119,72 @@ def tile_myinterleavedmodule_kernel(tc, x, W_dense, W_sparse, out):
                     nc.scalar.copy(out=dst, in_=src)
                 counts["banks"] += 1
             counts["transposed"] += 1
-
-        load_more()
-        for pair in range(2):
-            grps = {}
-            for mh in range(2):
-                m = 2 * pair + mh
-                transpose_tile(m, P, mh, 0, grps)
+            if key[0] == "x":
+                m = key[1]
                 nc.vector.quantize_mx(
-                    out=xcod[:, 512 * m : 512 * (m + 1)].bitcast(FP8X4),
-                    scales=xscl[:, 512 * m : 512 * (m + 1)],
-                    in_=grps[0][:, 2048 * mh : 2048 * (mh + 1)],
+                    out=xcod[m][:].bitcast(FP8X4),
+                    scales=xscl[m][:],
+                    in_=grps[(owner, 0)][:, 2048 * w : 2048 * (w + 1)],
                 )
-        load_more()
-
-        units = {}
-
-        def transpose_run(c):
-            n = CHUNKS[c]
-            grps = {}
-            idx = first_tile[c]
-            cods = {}
-            for w in range(2):
-                for s in range(n // P):
-                    transpose_tile(idx, n, w, s, grps)
-                    idx += 1
-                if n == P:
-                    if w == 0:
-                        cods[0] = (
-                            codp.tile([P, 1024], U32, name="cod", tag="cod", align_bytes=64),
-                            codp.tile([P, 1024], U8, name="scl", tag="scl", align_bytes=64),
-                        )
-                    nc.vector.quantize_mx(
-                        out=cods[0][0][:, 512 * w : 512 * (w + 1)].bitcast(FP8X4),
-                        scales=cods[0][1][:, 512 * w : 512 * (w + 1)],
-                        in_=grps[0][:, 2048 * w : 2048 * (w + 1)],
-                    )
-            if n != P:
-                for unit in range(8 * n // 1024):
-                    cods[unit] = (
-                        codp.tile([P, 1024], U32, name="cod", tag="cod", align_bytes=64),
-                        codp.tile([P, 1024], U8, name="scl", tag="scl", align_bytes=64),
-                    )
-                    nc.vector.quantize_mx(
-                        out=cods[unit][0][:].bitcast(FP8X4),
-                        scales=cods[unit][1][:],
-                        in_=grps[unit][:],
-                    )
-            units[c] = cods
+            elif n == P:
+                if w == 0:
+                    new_codes(owner, 0)
+                nc.vector.quantize_mx(
+                    out=cods[(owner, 0)][0][:, 512 * w : 512 * (w + 1)].bitcast(FP8X4),
+                    scales=cods[(owner, 0)][1][:, 512 * w : 512 * (w + 1)],
+                    in_=grps[(owner, 0)][:, 2048 * w : 2048 * (w + 1)],
+                )
+            elif s == n // P - 1:
+                for unit in range(4 * w // per_unit, 4 * (w + 1) // per_unit):
+                    pending.append((owner, unit))
             load_more()
 
-        starts = []
-        col0 = 0
-        for n in CHUNKS:
-            starts.append(col0)
-            col0 += n
-        ots = {}
-
-        def mx_run(c):
+        def mx_group(c, m):
+            flush_quantises()
             n = CHUNKS[c]
             per_unit = 1024 // n
             grp512 = starts[c] // 512
             off = starts[c] % 512
-            for m in range(4):
-                acc = apool.tile([P, 512], F32, name="acc", tag="acc")
-                for ag in range(8):
-                    g = ag % 4
-                    cod, scl = units[c][ag // per_unit]
-                    a = ag % per_unit
-                    xs = slice(512 * m + P * g, 512 * m + P * (g + 1))
-                    nc.tensor.matmul_mx(
-                        out=acc[:, 0:n],
-                        lhsT=xcod[:, xs].bitcast(FP8X4),
-                        lhsT_scale=xscl[:, xs],
-                        rhs=cod[:, a * n : (a + 1) * n].bitcast(FP8X4),
-                        rhs_scale=scl[:, a * n : (a + 1) * n],
-                        start=(ag == 0),
-                        stop=(ag == 7),
-                    )
-                if off == 0:
-                    ots[(grp512, m)] = otp.tile([P, 512], F32, name="ot", tag="ot")
-                ot = ots[(grp512, m)]
-                nc.scalar.copy(out=ot[:, off : off + n], in_=acc[:, 0:n])
-                if off + n == 512:
-                    nc.sync.dma_start(
-                        out=out[P * m : P * (m + 1), 512 * grp512 : 512 * (grp512 + 1)], in_=ot[:]
-                    )
+            acc = apool.tile([P, 512], F32, name="acc", tag="acc")
+            for ag in range(8):
+                g = ag % 4
+                cod, scl = cods[(c, ag // per_unit)]
+                a = ag % per_unit
+                xs = slice(P * g, P * (g + 1))
+                nc.tensor.matmul_mx(
+                    out=acc[:, 0:n],
+                    lhsT=xcod[m][:, xs].bitcast(FP8X4),
+                    lhsT_scale=xscl[m][:, xs],
+                    rhs=cod[:, a * n : (a + 1) * n].bitcast(FP8X4),
+                    rhs_scale=scl[:, a * n : (a + 1) * n],
+                    start=(ag == 0),
+                    stop=(ag == 7),
+                )
+            if off == 0:
+                ots[(grp512, m)] = otp.tile([P, 512], F32, name="ot", tag="ot")
+            ot = ots[(grp512, m)]
+            nc.scalar.copy(out=ot[:, off : off + n], in_=acc[:, 0:n])
+            if off + n == 512:
+                nc.sync.dma_start(
+                    out=out[P * m : P * (m + 1), 512 * grp512 : 512 * (grp512 + 1)], in_=ot[:]
+                )
 
-        transpose_run(0)
-        for c in range(len(CHUNKS)):
+        load_more()
+        transpose_tile(("x", 0, 0))
+        for key in chunk_tiles(0):
+            transpose_tile(key)
+        transpose_tile(("x", 1, 0))
+        transpose_tile(("x", 2, 0))
+        mx_group(0, 0)
+        transpose_tile(("x", 3, 0))
+        mx_group(0, 1)
+        mx_group(0, 2)
+        for key in chunk_tiles(1):
+            transpose_tile(key)
+        mx_group(0, 3)
+        for c in range(1, len(CHUNKS)):
             if c + 1 < len(CHUNKS):
-                transpose_run(c + 1)
-            mx_run(c)
+                for key in chunk_tiles(c + 1):
+                    transpose_tile(key)
+            for m in range(4):
+                mx_group(c, m)

@@ -23,6 +23,7 @@ OT_BUFS = 8
 T_BANKS = 6
 ACC_BANKS = 2
 V_EVERY = 2
+XPAD = 48
 
 
 def tile_myinterleavedmodule_kernel(tc, x, W_dense, W_sparse, out):
@@ -49,8 +50,8 @@ def tile_myinterleavedmodule_kernel(tc, x, W_dense, W_sparse, out):
 
         ident = const.tile([P, P], F32, name="ident")
         make_identity(nc, ident[:])
-        xcod = [const.tile([P, 512], U32, name="xcod%d" % m, align_bytes=64) for m in range(4)]
-        xscl = [const.tile([P, 512], U8, name="xscl%d" % m, align_bytes=64) for m in range(4)]
+        xcod = [const.tile([P, XPAD + 512], U32, name="xcod%d" % m, align_bytes=256) for m in range(4)]
+        xscl = [const.tile([P, 4 * 256], U8, name="xscl%d" % m, align_bytes=256) for m in range(4)]
 
         raw_tiles = {}
         counts = {"transposed": 0, "banks": 0, "flushed": 0}
@@ -73,8 +74,8 @@ def tile_myinterleavedmodule_kernel(tc, x, W_dense, W_sparse, out):
 
         def new_codes(c, unit):
             cods[(c, unit)] = (
-                codp.tile([P, 1024], U32, name="cod", tag="cod", align_bytes=64),
-                codp.tile([P, 1024], U8, name="scl", tag="scl", align_bytes=64),
+                codp.tile([P, 1024], U32, name="cod", tag="cod", align_bytes=256),
+                codp.tile([P, 1024], U8, name="scl", tag="scl", align_bytes=256),
             )
 
         def flush_quantises():
@@ -121,11 +122,12 @@ def tile_myinterleavedmodule_kernel(tc, x, W_dense, W_sparse, out):
             counts["transposed"] += 1
             if key[0] == "x":
                 m = key[1]
-                nc.vector.quantize_mx(
-                    out=xcod[m][:].bitcast(FP8X4),
-                    scales=xscl[m][:],
-                    in_=grps[(owner, 0)][:, 2048 * w : 2048 * (w + 1)],
-                )
+                for g in range(4):
+                    nc.vector.quantize_mx(
+                        out=xcod[m][:, XPAD + P * g : XPAD + P * (g + 1)].bitcast(FP8X4),
+                        scales=xscl[m][:, 256 * g : 256 * g + P],
+                        in_=grps[(owner, 0)][:, 2048 * w + 512 * g : 2048 * w + 512 * (g + 1)],
+                    )
             elif n == P:
                 if w == 0:
                     new_codes(owner, 0)
@@ -139,35 +141,49 @@ def tile_myinterleavedmodule_kernel(tc, x, W_dense, W_sparse, out):
                     pending.append((owner, unit))
             load_more()
 
-        def mx_group(c, m):
-            flush_quantises()
+        def mx_passes(c, m, lo, width):
             n = CHUNKS[c]
             per_unit = 1024 // n
-            grp512 = starts[c] // 512
-            off = starts[c] % 512
             acc = apool.tile([P, 512], F32, name="acc", tag="acc")
             for ag in range(8):
                 g = ag % 4
                 cod, scl = cods[(c, ag // per_unit)]
-                a = ag % per_unit
-                xs = slice(P * g, P * (g + 1))
+                cols = slice((ag % per_unit) * n + lo, (ag % per_unit) * n + lo + width)
                 nc.tensor.matmul_mx(
-                    out=acc[:, 0:n],
-                    lhsT=xcod[m][:, xs].bitcast(FP8X4),
-                    lhsT_scale=xscl[m][:, xs],
-                    rhs=cod[:, a * n : (a + 1) * n].bitcast(FP8X4),
-                    rhs_scale=scl[:, a * n : (a + 1) * n],
+                    out=acc[:, 0:width],
+                    lhsT=xcod[m][:, XPAD + P * g : XPAD + P * (g + 1)].bitcast(FP8X4),
+                    lhsT_scale=xscl[m][:, 256 * g : 256 * g + P],
+                    rhs=cod[:, cols].bitcast(FP8X4),
+                    rhs_scale=scl[:, cols],
                     start=(ag == 0),
                     stop=(ag == 7),
                 )
+            return acc
+
+        def mx_group(c, m):
+            flush_quantises()
+            n = CHUNKS[c]
+            grp512 = starts[c] // 512
+            off = starts[c] % 512
+            rows = slice(P * m, P * (m + 1))
+            if c == len(CHUNKS) - 1 and m == 3:
+                for h in range(2):
+                    acc = mx_passes(c, m, 256 * h, 256)
+                    ot = otp.tile([P, 256], F32, name="oth", tag="oth", bufs=2)
+                    if h == 0:
+                        nc.vector.tensor_copy(out=ot[:], in_=acc[:, 0:256])
+                    else:
+                        nc.scalar.copy(out=ot[:], in_=acc[:, 0:256])
+                    col0 = starts[c] + 256 * h
+                    nc.sync.dma_start(out=out[rows, col0 : col0 + 256], in_=ot[:])
+                return
+            acc = mx_passes(c, m, 0, n)
             if off == 0:
                 ots[(grp512, m)] = otp.tile([P, 512], F32, name="ot", tag="ot")
             ot = ots[(grp512, m)]
             nc.scalar.copy(out=ot[:, off : off + n], in_=acc[:, 0:n])
             if off + n == 512:
-                nc.sync.dma_start(
-                    out=out[P * m : P * (m + 1), 512 * grp512 : 512 * (grp512 + 1)], in_=ot[:]
-                )
+                nc.sync.dma_start(out=out[rows, 512 * grp512 : 512 * (grp512 + 1)], in_=ot[:])
 
         load_more()
         transpose_tile(("x", 0, 0))

@@ -15,7 +15,7 @@ K = 2048
 OUTS = 2048
 FLOPS = 2 * 2 * TOKENS * K * OUTS
 
-CHUNKS = (128, 128, 256, 256, 256, 512, 512)
+CHUNKS = (128, 128, 256, 256, 256, 256, 256, 256, 256)
 RAW_BUFS = 28
 GRP_BUFS = 4
 COD_BUFS = 8
@@ -166,16 +166,11 @@ def tile_myinterleavedmodule_kernel(tc, x, W_dense, W_sparse, out):
             grp512 = starts[c] // 512
             off = starts[c] % 512
             rows = slice(P * m, P * (m + 1))
-            if c == len(CHUNKS) - 1 and m == 3:
-                for h in range(2):
-                    acc = mx_passes(c, m, 256 * h, 256)
-                    ot = otp.tile([P, 256], F32, name="oth", tag="oth", bufs=2)
-                    if h == 0:
-                        nc.vector.tensor_copy(out=ot[:], in_=acc[:, 0:256])
-                    else:
-                        nc.scalar.copy(out=ot[:], in_=acc[:, 0:256])
-                    col0 = starts[c] + 256 * h
-                    nc.sync.dma_start(out=out[rows, col0 : col0 + 256], in_=ot[:])
+            if grp512 == 3 and m == 3:
+                acc = mx_passes(c, m, 0, n)
+                ot = otp.tile([P, 256], F32, name="oth", tag="oth", bufs=2)
+                nc.scalar.copy(out=ot[:], in_=acc[:, 0:n])
+                nc.sync.dma_start(out=out[rows, starts[c] : starts[c] + n], in_=ot[:])
                 return
             acc = mx_passes(c, m, 0, n)
             if off == 0:

@@ -15,187 +15,196 @@ K = 2048
 OUTS = 2048
 FLOPS = 2 * 2 * TOKENS * K * OUTS
 
-CHUNKS = (128, 128, 256, 256, 256, 256, 256, 256, 256)
+TOKEN_TILES = TOKENS // P
+PASSES = K // 512
+OPERANDS = 2 * PASSES
+BANK = 512
+SLAB = 1024
+
+CHUNKS = (128, 128, 256, 256, 256, 512, 512)
+
 RAW_BUFS = 28
-GRP_BUFS = 4
-COD_BUFS = 8
-OT_BUFS = 8
-T_BANKS = 6
-ACC_BANKS = 2
-V_EVERY = 2
-XPAD = 48
+SLAB_BUFS = 4
+CODE_BUFS = 8
+OUT_BUFS = 8
+GROUP_BANKS = 2
+TRANSPOSE_BANKS = 6
 
 
 def tile_myinterleavedmodule_kernel(tc, x, W_dense, W_sparse, out):
     nc = tc.nc
     weights = (W_dense, W_sparse)
-    starts = [sum(CHUNKS[:c]) for c in range(len(CHUNKS))]
+    chunk_start = [sum(CHUNKS[:c]) for c in range(len(CHUNKS))]
 
-    def chunk_tiles(c):
-        return [(c, w, s) for w in range(2) for s in range(CHUNKS[c] // P)]
+    def weight_tiles(c):
+        return [(c, w, b) for w in range(2) for b in range(CHUNKS[c] // P)]
 
-    load_order = [("x", 0, 0)] + chunk_tiles(0) + [("x", m, 0) for m in range(1, 4)]
+    def token_tile(m):
+        return ("x", m, 0)
+
+    load_order = [token_tile(0)] + weight_tiles(0) + [token_tile(m) for m in range(1, TOKEN_TILES)]
     for c in range(1, len(CHUNKS)):
-        load_order.extend(chunk_tiles(c))
+        load_order.extend(weight_tiles(c))
 
     with ExitStack() as ctx:
         const = ctx.enter_context(tc.tile_pool(name="const", bufs=1))
-        rawp = ctx.enter_context(tc.tile_pool(name="rawp", bufs=RAW_BUFS))
-        grpp = ctx.enter_context(tc.tile_pool(name="grpp", bufs=GRP_BUFS))
-        codp = ctx.enter_context(tc.tile_pool(name="codp", bufs=COD_BUFS))
-        otp = ctx.enter_context(tc.tile_pool(name="otp", bufs=OT_BUFS))
-        tpool = ctx.enter_context(tc.psum_pool(name="tpool", bufs=T_BANKS))
-        apool = ctx.enter_context(tc.psum_pool(name="apool", bufs=ACC_BANKS))
+        raw_pool = ctx.enter_context(tc.tile_pool(name="raw_pool", bufs=RAW_BUFS))
+        slab_pool = ctx.enter_context(tc.tile_pool(name="slab_pool", bufs=SLAB_BUFS))
+        code_pool = ctx.enter_context(tc.tile_pool(name="code_pool", bufs=CODE_BUFS))
+        out_pool = ctx.enter_context(tc.tile_pool(name="out_pool", bufs=OUT_BUFS))
+        transpose_psum = ctx.enter_context(tc.psum_pool(name="transpose_psum", bufs=TRANSPOSE_BANKS))
+        group_psum = ctx.enter_context(tc.psum_pool(name="group_psum", bufs=GROUP_BANKS))
         ctx.enter_context(tc.manual_schedule())
 
-        ident = const.tile([P, P], F32, name="ident")
-        make_identity(nc, ident[:])
-        xcod = [const.tile([P, XPAD + 512], U32, name="xcod%d" % m, align_bytes=256) for m in range(4)]
-        xscl = [const.tile([P, 4 * 256], U8, name="xscl%d" % m, align_bytes=256) for m in range(4)]
+        identity = const.tile([P, P], F32, name="identity")
+        make_identity(nc, identity[:])
+        x_codes = [const.tile([P, 512], U32, name="x_codes%d" % m, align_bytes=64) for m in range(TOKEN_TILES)]
+        x_scales = [const.tile([P, 512], U8, name="x_scales%d" % m, align_bytes=64) for m in range(TOKEN_TILES)]
 
         raw_tiles = {}
-        counts = {"transposed": 0, "banks": 0, "flushed": 0}
-        grps = {}
-        cods = {}
-        pending = []
-        ots = {}
+        slabs = {}
+        codes = {}
+        results = {}
+        waiting = []
+        count = {"transposed": 0, "banks": 0, "quantised": 0}
 
         def load_more():
-            while len(raw_tiles) < min(len(load_order), counts["transposed"] + RAW_BUFS):
-                key = load_order[len(raw_tiles)]
-                t = rawp.tile([P, K], BF16, name="raw", tag="raw")
-                if key[0] == "x":
-                    src = x[P * key[1] : P * (key[1] + 1), :]
+            while len(raw_tiles) < min(len(load_order), count["transposed"] + RAW_BUFS):
+                name = load_order[len(raw_tiles)]
+                if name[0] == "x":
+                    rows = x[P * name[1] : P * (name[1] + 1), :]
                 else:
-                    row0 = starts[key[0]] + P * key[2]
-                    src = weights[key[1]][row0 : row0 + P, :]
-                nc.sync.dma_start(out=t[:], in_=src)
-                raw_tiles[key] = t
+                    row0 = chunk_start[name[0]] + P * name[2]
+                    rows = weights[name[1]][row0 : row0 + P, :]
+                raw = raw_pool.tile([P, K], BF16, name="raw", tag="raw")
+                nc.sync.dma_start(out=raw[:], in_=rows)
+                raw_tiles[name] = raw
 
-        def new_codes(c, unit):
-            cods[(c, unit)] = (
-                codp.tile([P, 1024], U32, name="cod", tag="cod", align_bytes=256),
-                codp.tile([P, 1024], U8, name="scl", tag="scl", align_bytes=256),
+        def new_codes(c, number):
+            codes[(c, number)] = (
+                code_pool.tile([P, SLAB], U32, name="codes", tag="codes", align_bytes=64),
+                code_pool.tile([P, SLAB], U8, name="scales", tag="scales", align_bytes=64),
             )
 
-        def flush_quantises():
-            for c, unit in pending[counts["flushed"] :]:
-                new_codes(c, unit)
+        def quantise_waiting():
+            for c, number in waiting[count["quantised"] :]:
+                new_codes(c, number)
                 nc.vector.quantize_mx(
-                    out=cods[(c, unit)][0][:].bitcast(FP8X4),
-                    scales=cods[(c, unit)][1][:],
-                    in_=grps[(c, unit)][:],
+                    out=codes[(c, number)][0][:].bitcast(FP8X4),
+                    scales=codes[(c, number)][1][:],
+                    in_=slabs[(c, number)][:],
                 )
-            counts["flushed"] = len(pending)
+            count["quantised"] = len(waiting)
 
-        def transpose_tile(key):
-            if key[0] == "x":
-                owner, n, w, s = ("x", key[1] // 2), P, key[1] % 2, 0
+        def transpose_tile(name):
+            if name[0] == "x":
+                owner, n, w, block = ("x", name[1] // 2), P, name[1] % 2, 0
             else:
-                owner, n, w, s = key[0], CHUNKS[key[0]], key[1], key[2]
-            per_unit = 1024 // n
-            rawf = raw_tiles[key][:].bitcast(F32)
-            for gp in range(2):
-                ag = 4 * w + 2 * gp
-                unit = ag // per_unit
-                a0 = ag % per_unit
-                if (owner, unit) not in grps:
-                    grps[(owner, unit)] = grpp.tile([P, 4096], BF16, name="grp", tag="grp", align_bytes=64)
-                tp = tpool.tile([P, 512], F32, name="tp", tag="tp")
+                owner, n, w, block = name[0], CHUNKS[name[0]], name[1], name[2]
+            per_slab = SLAB // n
+            pairs = raw_tiles[name][:].bitcast(F32)
+            for half in range(2):
+                operand = PASSES * w + 2 * half
+                number = operand // per_slab
+                if (owner, number) not in slabs:
+                    slabs[(owner, number)] = slab_pool.tile(
+                        [P, 4 * SLAB], BF16, name="slab", tag="slab", align_bytes=64
+                    )
+                bank = transpose_psum.tile([P, BANK], F32, name="bank", tag="bank")
                 for q in range(4):
-                    j = 4 * gp + q
+                    j = 4 * half + q
                     nc.tensor.transpose(
-                        out=tp[:, P * q : P * (q + 1)],
-                        in_=rawf[:, P * j : P * (j + 1)],
-                        identity=ident[:],
+                        out=bank[:, P * q : P * (q + 1)],
+                        in_=pairs[:, P * j : P * (j + 1)],
+                        identity=identity[:],
                     )
-                src = tp[:].rearrange("p (g u o) -> p g o u", g=2, u=2)
-                grpf = grps[(owner, unit)][:].bitcast(F32).rearrange(
-                    "p (a o u) -> p a o u", a=per_unit, o=n, u=2
+                planes = bank[:].rearrange("p (g u r) -> p g r u", g=2, u=2)
+                slab_pairs = slabs[(owner, number)][:].bitcast(F32).rearrange(
+                    "p (a r u) -> p a r u", a=per_slab, r=n, u=2
                 )
-                dst = grpf[:, a0 : a0 + 2, P * s : P * (s + 1), :]
-                if counts["banks"] % V_EVERY == V_EVERY - 1:
-                    nc.vector.tensor_copy(out=dst, in_=src)
+                first = operand % per_slab
+                regrouped = slab_pairs[:, first : first + 2, P * block : P * (block + 1), :]
+                if count["banks"] % 2 == 0:
+                    nc.scalar.copy(out=regrouped, in_=planes)
                 else:
-                    nc.scalar.copy(out=dst, in_=src)
-                counts["banks"] += 1
-            counts["transposed"] += 1
-            if key[0] == "x":
-                m = key[1]
-                for g in range(4):
-                    nc.vector.quantize_mx(
-                        out=xcod[m][:, XPAD + P * g : XPAD + P * (g + 1)].bitcast(FP8X4),
-                        scales=xscl[m][:, 256 * g : 256 * g + P],
-                        in_=grps[(owner, 0)][:, 2048 * w + 512 * g : 2048 * w + 512 * (g + 1)],
-                    )
-            elif n == P:
-                if w == 0:
-                    new_codes(owner, 0)
+                    nc.vector.tensor_copy(out=regrouped, in_=planes)
+                count["banks"] += 1
+            count["transposed"] += 1
+            if n == P:
+                if name[0] == "x":
+                    words, scale_bytes = x_codes[name[1]][:], x_scales[name[1]][:]
+                else:
+                    if w == 0:
+                        new_codes(owner, 0)
+                    words = codes[(owner, 0)][0][:, 512 * w : 512 * (w + 1)]
+                    scale_bytes = codes[(owner, 0)][1][:, 512 * w : 512 * (w + 1)]
                 nc.vector.quantize_mx(
-                    out=cods[(owner, 0)][0][:, 512 * w : 512 * (w + 1)].bitcast(FP8X4),
-                    scales=cods[(owner, 0)][1][:, 512 * w : 512 * (w + 1)],
-                    in_=grps[(owner, 0)][:, 2048 * w : 2048 * (w + 1)],
+                    out=words.bitcast(FP8X4),
+                    scales=scale_bytes,
+                    in_=slabs[(owner, 0)][:, 2048 * w : 2048 * (w + 1)],
                 )
-            elif s == n // P - 1:
-                for unit in range(4 * w // per_unit, 4 * (w + 1) // per_unit):
-                    pending.append((owner, unit))
+            elif block == n // P - 1:
+                for number in range(PASSES * w // per_slab, PASSES * (w + 1) // per_slab):
+                    waiting.append((owner, number))
             load_more()
 
-        def mx_passes(c, m, lo, width):
+        def passes(c, m, first_col, width):
             n = CHUNKS[c]
-            per_unit = 1024 // n
-            acc = apool.tile([P, 512], F32, name="acc", tag="acc")
-            for ag in range(8):
-                g = ag % 4
-                cod, scl = cods[(c, ag // per_unit)]
-                cols = slice((ag % per_unit) * n + lo, (ag % per_unit) * n + lo + width)
+            per_slab = SLAB // n
+            sums = group_psum.tile([P, BANK], F32, name="sums", tag="sums")
+            for operand in range(OPERANDS):
+                g = operand % PASSES
+                words, scale_bytes = codes[(c, operand // per_slab)]
+                col0 = (operand % per_slab) * n + first_col
                 nc.tensor.matmul_mx(
-                    out=acc[:, 0:width],
-                    lhsT=xcod[m][:, XPAD + P * g : XPAD + P * (g + 1)].bitcast(FP8X4),
-                    lhsT_scale=xscl[m][:, 256 * g : 256 * g + P],
-                    rhs=cod[:, cols].bitcast(FP8X4),
-                    rhs_scale=scl[:, cols],
-                    start=(ag == 0),
-                    stop=(ag == 7),
+                    out=sums[:, 0:width],
+                    lhsT=x_codes[m][:, P * g : P * (g + 1)].bitcast(FP8X4),
+                    lhsT_scale=x_scales[m][:, P * g : P * (g + 1)],
+                    rhs=words[:, col0 : col0 + width].bitcast(FP8X4),
+                    rhs_scale=scale_bytes[:, col0 : col0 + width],
+                    start=(operand == 0),
+                    stop=(operand == OPERANDS - 1),
                 )
-            return acc
+            return sums
 
-        def mx_group(c, m):
-            flush_quantises()
+        def group(c, m):
+            quantise_waiting()
             n = CHUNKS[c]
-            grp512 = starts[c] // 512
-            off = starts[c] % 512
-            rows = slice(P * m, P * (m + 1))
-            if grp512 == 3 and m == 3:
-                acc = mx_passes(c, m, 0, n)
-                ot = otp.tile([P, 256], F32, name="oth", tag="oth", bufs=2)
-                nc.scalar.copy(out=ot[:], in_=acc[:, 0:n])
-                nc.sync.dma_start(out=out[rows, starts[c] : starts[c] + n], in_=ot[:])
+            token_rows = slice(P * m, P * (m + 1))
+            if c == len(CHUNKS) - 1 and m == TOKEN_TILES - 1:
+                for h in range(2):
+                    sums = passes(c, m, h * n // 2, n // 2)
+                    part = out_pool.tile([P, n // 2], F32, name="part", tag="part", bufs=2)
+                    if h == 0:
+                        nc.vector.tensor_copy(out=part[:], in_=sums[:, 0 : n // 2])
+                    else:
+                        nc.scalar.copy(out=part[:], in_=sums[:, 0 : n // 2])
+                    col0 = chunk_start[c] + h * n // 2
+                    nc.sync.dma_start(out=out[token_rows, col0 : col0 + n // 2], in_=part[:])
                 return
-            acc = mx_passes(c, m, 0, n)
-            if off == 0:
-                ots[(grp512, m)] = otp.tile([P, 512], F32, name="ot", tag="ot")
-            ot = ots[(grp512, m)]
-            nc.scalar.copy(out=ot[:, off : off + n], in_=acc[:, 0:n])
-            if off + n == 512:
-                nc.sync.dma_start(out=out[rows, 512 * grp512 : 512 * (grp512 + 1)], in_=ot[:])
+            sums = passes(c, m, 0, n)
+            col_range, offset = divmod(chunk_start[c], BANK)
+            if offset == 0:
+                results[(col_range, m)] = out_pool.tile([P, BANK], F32, name="result", tag="result")
+            result = results[(col_range, m)]
+            nc.scalar.copy(out=result[:, offset : offset + n], in_=sums[:, 0:n])
+            if offset + n == BANK:
+                nc.sync.dma_start(out=out[token_rows, BANK * col_range : BANK * (col_range + 1)], in_=result[:])
 
         load_more()
-        transpose_tile(("x", 0, 0))
-        for key in chunk_tiles(0):
-            transpose_tile(key)
-        transpose_tile(("x", 1, 0))
-        transpose_tile(("x", 2, 0))
-        mx_group(0, 0)
-        transpose_tile(("x", 3, 0))
-        mx_group(0, 1)
-        mx_group(0, 2)
-        for key in chunk_tiles(1):
-            transpose_tile(key)
-        mx_group(0, 3)
+
+        for name in [token_tile(0)] + weight_tiles(0) + [token_tile(1), token_tile(2)]:
+            transpose_tile(name)
+        group(0, 0)
+        group(0, 1)
+        for name in [token_tile(3)] + weight_tiles(1):
+            transpose_tile(name)
+        group(0, 2)
+        group(0, 3)
+
         for c in range(1, len(CHUNKS)):
             if c + 1 < len(CHUNKS):
-                for key in chunk_tiles(c + 1):
-                    transpose_tile(key)
-            for m in range(4):
-                mx_group(c, m)
+                for name in weight_tiles(c + 1):
+                    transpose_tile(name)
+            for m in range(TOKEN_TILES):
+                group(c, m)

@@ -16,10 +16,16 @@ OUTS = 2048
 FLOPS = 2 * 2 * TOKENS * K * OUTS
 
 TOKEN_TILES = TOKENS // P
-PASSES = K // 512
+PACK = 4
+PASSES = K // (PACK * P)
 OPERANDS = 2 * PASSES
 BANK = 512
+PER_BANK = BANK // P
 SLAB = 1024
+
+ALIGN = 256
+X_PAD = 48
+X_SCALE_SLOT = 256
 
 CHUNKS = (128, 128, 256, 256, 256, 512, 512)
 
@@ -37,7 +43,7 @@ def tile_myinterleavedmodule_kernel(tc, x, W_dense, W_sparse, out):
     chunk_start = [sum(CHUNKS[:c]) for c in range(len(CHUNKS))]
 
     def weight_tiles(c):
-        return [(c, w, b) for w in range(2) for b in range(CHUNKS[c] // P)]
+        return [(c, w, strip) for w in range(2) for strip in range(CHUNKS[c] // P)]
 
     def token_tile(m):
         return ("x", m, 0)
@@ -58,8 +64,20 @@ def tile_myinterleavedmodule_kernel(tc, x, W_dense, W_sparse, out):
 
         identity = const.tile([P, P], F32, name="identity")
         make_identity(nc, identity[:])
-        x_codes = [const.tile([P, 512], U32, name="x_codes%d" % m, align_bytes=64) for m in range(TOKEN_TILES)]
-        x_scales = [const.tile([P, 512], U8, name="x_scales%d" % m, align_bytes=64) for m in range(TOKEN_TILES)]
+        x_codes = [
+            const.tile([P, X_PAD + PASSES * P], U32, name="x_codes%d" % m, align_bytes=ALIGN)
+            for m in range(TOKEN_TILES)
+        ]
+        x_scales = [
+            const.tile([P, PASSES * X_SCALE_SLOT], U8, name="x_scales%d" % m, align_bytes=ALIGN)
+            for m in range(TOKEN_TILES)
+        ]
+
+        def x_operand(m, g):
+            return (
+                x_codes[m][:, X_PAD + P * g : X_PAD + P * (g + 1)],
+                x_scales[m][:, X_SCALE_SLOT * g : X_SCALE_SLOT * g + P],
+            )
 
         raw_tiles = {}
         slabs = {}
@@ -82,8 +100,8 @@ def tile_myinterleavedmodule_kernel(tc, x, W_dense, W_sparse, out):
 
         def new_codes(c, number):
             codes[(c, number)] = (
-                code_pool.tile([P, SLAB], U32, name="codes", tag="codes", align_bytes=64),
-                code_pool.tile([P, SLAB], U8, name="scales", tag="scales", align_bytes=64),
+                code_pool.tile([P, SLAB], U32, name="codes", tag="codes", align_bytes=ALIGN),
+                code_pool.tile([P, SLAB], U8, name="scales", tag="scales", align_bytes=ALIGN),
             )
 
         def quantise_waiting():
@@ -98,21 +116,21 @@ def tile_myinterleavedmodule_kernel(tc, x, W_dense, W_sparse, out):
 
         def transpose_tile(name):
             if name[0] == "x":
-                owner, n, w, block = ("x", name[1] // 2), P, name[1] % 2, 0
+                owner, n, w, strip = ("x", name[1] // 2), P, name[1] % 2, 0
             else:
-                owner, n, w, block = name[0], CHUNKS[name[0]], name[1], name[2]
+                owner, n, w, strip = name[0], CHUNKS[name[0]], name[1], name[2]
             per_slab = SLAB // n
             pairs = raw_tiles[name][:].bitcast(F32)
-            for half in range(2):
-                operand = PASSES * w + 2 * half
+            for first_pass in range(0, PASSES, 2):
+                operand = PASSES * w + first_pass
                 number = operand // per_slab
                 if (owner, number) not in slabs:
                     slabs[(owner, number)] = slab_pool.tile(
-                        [P, 4 * SLAB], BF16, name="slab", tag="slab", align_bytes=64
+                        [P, PACK * SLAB], BF16, name="slab", tag="slab", align_bytes=64
                     )
                 bank = transpose_psum.tile([P, BANK], F32, name="bank", tag="bank")
-                for q in range(4):
-                    j = 4 * half + q
+                for q in range(PER_BANK):
+                    j = 2 * first_pass + q
                     nc.tensor.transpose(
                         out=bank[:, P * q : P * (q + 1)],
                         in_=pairs[:, P * j : P * (j + 1)],
@@ -123,27 +141,31 @@ def tile_myinterleavedmodule_kernel(tc, x, W_dense, W_sparse, out):
                     "p (a r u) -> p a r u", a=per_slab, r=n, u=2
                 )
                 first = operand % per_slab
-                regrouped = slab_pairs[:, first : first + 2, P * block : P * (block + 1), :]
+                regrouped = slab_pairs[:, first : first + 2, P * strip : P * (strip + 1), :]
                 if count["banks"] % 2 == 0:
                     nc.scalar.copy(out=regrouped, in_=planes)
                 else:
                     nc.vector.tensor_copy(out=regrouped, in_=planes)
                 count["banks"] += 1
             count["transposed"] += 1
-            if n == P:
-                if name[0] == "x":
-                    words, scale_bytes = x_codes[name[1]][:], x_scales[name[1]][:]
-                else:
-                    if w == 0:
-                        new_codes(owner, 0)
-                    words = codes[(owner, 0)][0][:, 512 * w : 512 * (w + 1)]
-                    scale_bytes = codes[(owner, 0)][1][:, 512 * w : 512 * (w + 1)]
+            word0 = PASSES * P * w
+            if name[0] == "x":
+                for g in range(PASSES):
+                    words, scale_bytes = x_operand(name[1], g)
+                    nc.vector.quantize_mx(
+                        out=words.bitcast(FP8X4),
+                        scales=scale_bytes,
+                        in_=slabs[(owner, 0)][:, PACK * (word0 + P * g) : PACK * (word0 + P * (g + 1))],
+                    )
+            elif n == P:
+                if w == 0:
+                    new_codes(owner, 0)
                 nc.vector.quantize_mx(
-                    out=words.bitcast(FP8X4),
-                    scales=scale_bytes,
-                    in_=slabs[(owner, 0)][:, 2048 * w : 2048 * (w + 1)],
+                    out=codes[(owner, 0)][0][:, word0 : word0 + PASSES * P].bitcast(FP8X4),
+                    scales=codes[(owner, 0)][1][:, word0 : word0 + PASSES * P],
+                    in_=slabs[(owner, 0)][:, PACK * word0 : PACK * (word0 + PASSES * P)],
                 )
-            elif block == n // P - 1:
+            elif strip == n // P - 1:
                 for number in range(PASSES * w // per_slab, PASSES * (w + 1) // per_slab):
                     waiting.append((owner, number))
             load_more()
@@ -153,13 +175,13 @@ def tile_myinterleavedmodule_kernel(tc, x, W_dense, W_sparse, out):
             per_slab = SLAB // n
             sums = group_psum.tile([P, BANK], F32, name="sums", tag="sums")
             for operand in range(OPERANDS):
-                g = operand % PASSES
+                x_words, x_scale_bytes = x_operand(m, operand % PASSES)
                 words, scale_bytes = codes[(c, operand // per_slab)]
                 col0 = (operand % per_slab) * n + first_col
                 nc.tensor.matmul_mx(
                     out=sums[:, 0:width],
-                    lhsT=x_codes[m][:, P * g : P * (g + 1)].bitcast(FP8X4),
-                    lhsT_scale=x_scales[m][:, P * g : P * (g + 1)],
+                    lhsT=x_words.bitcast(FP8X4),
+                    lhsT_scale=x_scale_bytes,
                     rhs=words[:, col0 : col0 + width].bitcast(FP8X4),
                     rhs_scale=scale_bytes[:, col0 : col0 + width],
                     start=(operand == 0),
@@ -196,10 +218,11 @@ def tile_myinterleavedmodule_kernel(tc, x, W_dense, W_sparse, out):
         for name in [token_tile(0)] + weight_tiles(0) + [token_tile(1), token_tile(2)]:
             transpose_tile(name)
         group(0, 0)
+        transpose_tile(token_tile(3))
         group(0, 1)
-        for name in [token_tile(3)] + weight_tiles(1):
-            transpose_tile(name)
         group(0, 2)
+        for name in weight_tiles(1):
+            transpose_tile(name)
         group(0, 3)
 
         for c in range(1, len(CHUNKS)):

from contextlib import ExitStack

import concourse.mybir as mybir
from concourse.masks import make_identity

FP8X4 = mybir.dt.float8_e4m3fn_x4
BF16 = mybir.dt.bfloat16
F32 = mybir.dt.float32
U32 = mybir.dt.uint32
U8 = mybir.dt.uint8

P = 128
TOKENS = 512
K = 2048
OUTS = 2048
FLOPS = 2 * 2 * TOKENS * K * OUTS

TOKEN_TILES = TOKENS // P
PACK = 4
PASSES = K // (PACK * P)
OPERANDS = 2 * PASSES
BANK = 512
PER_BANK = BANK // P
SLAB = 1024

ALIGN = 256
X_PAD = 48
X_SCALE_SLOT = 256

CHUNKS = (128, 128, 256, 256, 256, 512, 512)

RAW_BUFS = 28
SLAB_BUFS = 4
CODE_BUFS = 8
OUT_BUFS = 8
GROUP_BANKS = 2
TRANSPOSE_BANKS = 6


def tile_myinterleavedmodule_kernel(tc, x, W_dense, W_sparse, out):
    nc = tc.nc
    weights = (W_dense, W_sparse)
    chunk_start = [sum(CHUNKS[:c]) for c in range(len(CHUNKS))]

    def weight_tiles(c):
        return [(c, w, strip) for w in range(2) for strip in range(CHUNKS[c] // P)]

    def token_tile(m):
        return ("x", m, 0)

    load_order = [token_tile(0)] + weight_tiles(0) + [token_tile(m) for m in range(1, TOKEN_TILES)]
    for c in range(1, len(CHUNKS)):
        load_order.extend(weight_tiles(c))

    with ExitStack() as ctx:
        const = ctx.enter_context(tc.tile_pool(name="const", bufs=1))
        raw_pool = ctx.enter_context(tc.tile_pool(name="raw_pool", bufs=RAW_BUFS))
        slab_pool = ctx.enter_context(tc.tile_pool(name="slab_pool", bufs=SLAB_BUFS))
        code_pool = ctx.enter_context(tc.tile_pool(name="code_pool", bufs=CODE_BUFS))
        out_pool = ctx.enter_context(tc.tile_pool(name="out_pool", bufs=OUT_BUFS))
        transpose_psum = ctx.enter_context(tc.psum_pool(name="transpose_psum", bufs=TRANSPOSE_BANKS))
        group_psum = ctx.enter_context(tc.psum_pool(name="group_psum", bufs=GROUP_BANKS))
        ctx.enter_context(tc.manual_schedule())

        identity = const.tile([P, P], F32, name="identity")
        make_identity(nc, identity[:])
        x_codes = [
            const.tile([P, X_PAD + PASSES * P], U32, name="x_codes%d" % m, align_bytes=ALIGN)
            for m in range(TOKEN_TILES)
        ]
        x_scales = [
            const.tile([P, PASSES * X_SCALE_SLOT], U8, name="x_scales%d" % m, align_bytes=ALIGN)
            for m in range(TOKEN_TILES)
        ]

        def x_operand(m, g):
            return (
                x_codes[m][:, X_PAD + P * g : X_PAD + P * (g + 1)],
                x_scales[m][:, X_SCALE_SLOT * g : X_SCALE_SLOT * g + P],
            )

        raw_tiles = {}
        slabs = {}
        codes = {}
        results = {}
        waiting = []
        count = {"transposed": 0, "banks": 0, "quantised": 0}

        def load_more():
            while len(raw_tiles) < min(len(load_order), count["transposed"] + RAW_BUFS):
                name = load_order[len(raw_tiles)]
                if name[0] == "x":
                    rows = x[P * name[1] : P * (name[1] + 1), :]
                else:
                    row0 = chunk_start[name[0]] + P * name[2]
                    rows = weights[name[1]][row0 : row0 + P, :]
                raw = raw_pool.tile([P, K], BF16, name="raw", tag="raw")
                nc.sync.dma_start(out=raw[:], in_=rows)
                raw_tiles[name] = raw

        def new_codes(c, number):
            codes[(c, number)] = (
                code_pool.tile([P, SLAB], U32, name="codes", tag="codes", align_bytes=ALIGN),
                code_pool.tile([P, SLAB], U8, name="scales", tag="scales", align_bytes=ALIGN),
            )

        def quantise_waiting():
            for c, number in waiting[count["quantised"] :]:
                new_codes(c, number)
                nc.vector.quantize_mx(
                    out=codes[(c, number)][0][:].bitcast(FP8X4),
                    scales=codes[(c, number)][1][:],
                    in_=slabs[(c, number)][:],
                )
            count["quantised"] = len(waiting)

        def transpose_tile(name):
            if name[0] == "x":
                owner, n, w, strip = ("x", name[1] // 2), P, name[1] % 2, 0
            else:
                owner, n, w, strip = name[0], CHUNKS[name[0]], name[1], name[2]
            per_slab = SLAB // n
            pairs = raw_tiles[name][:].bitcast(F32)
            for first_pass in range(0, PASSES, 2):
                operand = PASSES * w + first_pass
                number = operand // per_slab
                if (owner, number) not in slabs:
                    slabs[(owner, number)] = slab_pool.tile(
                        [P, PACK * SLAB], BF16, name="slab", tag="slab", align_bytes=64
                    )
                bank = transpose_psum.tile([P, BANK], F32, name="bank", tag="bank")
                for q in range(PER_BANK):
                    j = 2 * first_pass + q
                    nc.tensor.transpose(
                        out=bank[:, P * q : P * (q + 1)],
                        in_=pairs[:, P * j : P * (j + 1)],
                        identity=identity[:],
                    )
                planes = bank[:].rearrange("p (g u r) -> p g r u", g=2, u=2)
                slab_pairs = slabs[(owner, number)][:].bitcast(F32).rearrange(
                    "p (a r u) -> p a r u", a=per_slab, r=n, u=2
                )
                first = operand % per_slab
                regrouped = slab_pairs[:, first : first + 2, P * strip : P * (strip + 1), :]
                if count["banks"] % 2 == 0:
                    nc.scalar.copy(out=regrouped, in_=planes)
                else:
                    nc.vector.tensor_copy(out=regrouped, in_=planes)
                count["banks"] += 1
            count["transposed"] += 1
            word0 = PASSES * P * w
            if name[0] == "x":
                for g in range(PASSES):
                    words, scale_bytes = x_operand(name[1], g)
                    nc.vector.quantize_mx(
                        out=words.bitcast(FP8X4),
                        scales=scale_bytes,
                        in_=slabs[(owner, 0)][:, PACK * (word0 + P * g) : PACK * (word0 + P * (g + 1))],
                    )
            elif n == P:
                if w == 0:
                    new_codes(owner, 0)
                nc.vector.quantize_mx(
                    out=codes[(owner, 0)][0][:, word0 : word0 + PASSES * P].bitcast(FP8X4),
                    scales=codes[(owner, 0)][1][:, word0 : word0 + PASSES * P],
                    in_=slabs[(owner, 0)][:, PACK * word0 : PACK * (word0 + PASSES * P)],
                )
            elif strip == n // P - 1:
                for number in range(PASSES * w // per_slab, PASSES * (w + 1) // per_slab):
                    waiting.append((owner, number))
            load_more()

        def passes(c, m, first_col, width):
            n = CHUNKS[c]
            per_slab = SLAB // n
            sums = group_psum.tile([P, BANK], F32, name="sums", tag="sums")
            for operand in range(OPERANDS):
                x_words, x_scale_bytes = x_operand(m, operand % PASSES)
                words, scale_bytes = codes[(c, operand // per_slab)]
                col0 = (operand % per_slab) * n + first_col
                nc.tensor.matmul_mx(
                    out=sums[:, 0:width],
                    lhsT=x_words.bitcast(FP8X4),
                    lhsT_scale=x_scale_bytes,
                    rhs=words[:, col0 : col0 + width].bitcast(FP8X4),
                    rhs_scale=scale_bytes[:, col0 : col0 + width],
                    start=(operand == 0),
                    stop=(operand == OPERANDS - 1),
                )
            return sums

        def group(c, m):
            quantise_waiting()
            n = CHUNKS[c]
            token_rows = slice(P * m, P * (m + 1))
            if c == len(CHUNKS) - 1 and m == TOKEN_TILES - 1:
                for h in range(2):
                    sums = passes(c, m, h * n // 2, n // 2)
                    part = out_pool.tile([P, n // 2], F32, name="part", tag="part", bufs=2)
                    if h == 0:
                        nc.vector.tensor_copy(out=part[:], in_=sums[:, 0 : n // 2])
                    else:
                        nc.scalar.copy(out=part[:], in_=sums[:, 0 : n // 2])
                    col0 = chunk_start[c] + h * n // 2
                    nc.sync.dma_start(out=out[token_rows, col0 : col0 + n // 2], in_=part[:])
                return
            sums = passes(c, m, 0, n)
            col_range, offset = divmod(chunk_start[c], BANK)
            if offset == 0:
                results[(col_range, m)] = out_pool.tile([P, BANK], F32, name="result", tag="result")
            result = results[(col_range, m)]
            nc.scalar.copy(out=result[:, offset : offset + n], in_=sums[:, 0:n])
            if offset + n == BANK:
                nc.sync.dma_start(out=out[token_rows, BANK * col_range : BANK * (col_range + 1)], in_=result[:])

        load_more()

        for name in [token_tile(0)] + weight_tiles(0) + [token_tile(1), token_tile(2)]:
            transpose_tile(name)
        group(0, 0)
        transpose_tile(token_tile(3))
        group(0, 1)
        group(0, 2)
        for name in weight_tiles(1):
            transpose_tile(name)
        group(0, 3)

        for c in range(1, len(CHUNKS)):
            if c + 1 < len(CHUNKS):
                for name in weight_tiles(c + 1):
                    transpose_tile(name)
            for m in range(TOKEN_TILES):
                group(c, m)
